import numpy as np
import ml_dtypes


def mxq(x, axis, fmt="e4m3"):
    dtype, down = {"e4m3": (ml_dtypes.float8_e4m3fn, 7), "e5m2": (ml_dtypes.float8_e5m2, 14)}[fmt]
    v = np.moveaxis(np.asarray(x, np.float32).astype(ml_dtypes.bfloat16).astype(np.float64), axis, -1)
    blocks = v.reshape(v.shape[:-1] + (-1, 32))
    amax = np.abs(blocks).max(-1, keepdims=True)
    byte = np.maximum(np.where(amax > 0, np.frexp(amax)[1] - 1 + 127, 0) - down, 1)
    scale = np.exp2(byte - 127.0)
    codes = (blocks / scale).astype(np.float32).astype(dtype).astype(np.float64)
    return np.moveaxis((codes * scale).reshape(v.shape), -1, axis)


WIDE = False


def mx_kscale(k):
    if not WIDE:
        return np.ones(k)
    levels = np.array([10, -10, 5, -5, 0])
    a = np.random.permutation(np.resize(levels, k // 512 * 4)).reshape(k // 512, 4)
    idx = np.arange(k)
    return np.exp2(a[idx // 512, idx % 128 // 32])


BF16 = ml_dtypes.bfloat16


def bf(x):
    return np.asarray(x, np.float32).astype(BF16)


def f64(x):
    return np.asarray(x).astype(np.float64)


E2M1 = np.array([0.0, 0.5, 1.0, 1.5, 2.0, 3.0, 4.0, 6.0, -0.0, -0.5, -1.0, -1.5, -2.0, -3.0, -4.0, -6.0])


def pack_weight(w, fmt):
    k, n = w.shape
    w = f64(bf(w)).reshape(k // 32, 32, n)
    amax = np.abs(w).max(1)
    if fmt == "e4m3":
        byte = np.frexp(amax)[1] - 1 + 127 - 7
    else:
        mant, ex = np.frexp(amax / 6.0)
        byte = np.where(mant > 0.5, ex, ex - 1) + 127
    byte = np.clip(np.where(amax > 0, byte, 1), 1, 254)
    scaled = (w * np.exp2(127.0 - byte)[:, None, :]).reshape(k, n).astype(np.float32)
    by_word = np.ascontiguousarray(scaled.reshape(k // 512, 128, 4, n).transpose(0, 1, 3, 2))
    if fmt == "e4m3":
        words = by_word.astype(ml_dtypes.float8_e4m3fn).view(np.uint8)
    else:
        c = by_word.astype(ml_dtypes.float4_e2m1fn).view(np.uint8) & 0xF
        words = c[..., 0::2] | (c[..., 1::2] << 4)
    return np.ascontiguousarray(words), np.ascontiguousarray(byte.astype(np.uint8).reshape(k // 512, 16, n))


def unpack_weight(words, scales, fmt):
    g, p, n, _ = words.shape
    if fmt == "e4m3":
        vals = np.ascontiguousarray(words).view(ml_dtypes.float8_e4m3fn).astype(np.float64)
    else:
        nib = np.empty((g, p, n, 4), np.uint8)
        nib[..., 0::2] = words & 0xF
        nib[..., 1::2] = words >> 4
        vals = E2M1[nib]
    vals = vals * np.repeat(np.exp2(scales.astype(np.float64) - 127.0), 8, axis=1)[..., None]
    return vals.transpose(0, 1, 3, 2).reshape(g * 512, n)


B, T, L, D, K = 4, 512, 256, 1024, 128
HS = 0.25
FMT = "e4m3"


def sigmoid(v):
    return 1.0 / (1.0 + np.exp(-v))


def setup_inputs():
    s = mx_kscale(D)
    H = bf(np.random.standard_normal((B, T, D)) * HS * s)
    Wr = np.random.standard_normal((K, D)) / (HS * np.sqrt(D)) / s
    words, scales = pack_weight(np.ascontiguousarray(Wr.T), FMT)
    br = bf(np.random.standard_normal(K) * 0.3)
    return {"H": H, "Wr_words": words, "Wr_scales": scales, "br": br}


def reference(H, Wr_words, Wr_scales, br):
    h = f64(H)
    route = sigmoid((mxq(h, 2, "e4m3") @ unpack_weight(Wr_words, Wr_scales, FMT)) + f64(br))
    return mxq(route, 1, "e4m3").transpose(0, 2, 1) @ mxq(h, 1, "e4m3")

@@ -1,0 +1,163 @@
+from contextlib import ExitStack
+
+import concourse.mybir as mybir
+from concourse.masks import make_identity
+
+F32 = mybir.dt.float32
+BF16 = mybir.dt.bfloat16
+I32 = mybir.dt.int32
+U32 = mybir.dt.uint32
+U8 = mybir.dt.uint8
+FP8X4 = mybir.dt.float8_e4m3fn_x4
+
+P = 128
+PACK = 4
+K_PASS = P * PACK
+
+SEQS, FRAMES, FEATURES, SLOTS = 4, 512, 1024, 128
+HALVES = FEATURES // K_PASS
+UNITS = SEQS * HALVES
+PAIRS = K_PASS // 2
+
+SCALAR_SHARE = K_PASS // 4
+VECTOR_SHARE = K_PASS - SCALAR_SHARE
+RUN = 4
+
+FLOPS = 2 * (2 * SEQS * FRAMES * FEATURES * SLOTS)
+
+
+def tile_instrumentspecificslotmemory_pa_kernel(tc, H, Wr_words, Wr_scales, br, out):
+    nc = tc.nc
+    with ExitStack() as ctx:
+        const = ctx.enter_context(tc.tile_pool(name="const", bufs=1))
+        per_unit = ctx.enter_context(tc.tile_pool(name="per_unit", bufs=UNITS))
+        per_seq = ctx.enter_context(tc.tile_pool(name="per_seq", bufs=SEQS))
+        psum_t = ctx.enter_context(tc.psum_pool(name="psum_t", bufs=4))
+        psum_r = ctx.enter_context(tc.psum_pool(name="psum_r", bufs=2))
+        psum_a = ctx.enter_context(tc.psum_pool(name="psum_a", bufs=2))
+
+        identity = const.tile([P, P], F32)
+        make_identity(nc, identity[:])
+
+        zero = const.tile([P, 1], F32)
+        half = const.tile([P, 1], F32)
+        nc.vector.memset(zero[:], 0.0)
+        nc.scalar.activation(out=half[:], in_=zero[:], func=mybir.ActivationFunctionType.Sigmoid)
+
+        w_codes = const.tile([P, HALVES, SLOTS], U32, align_bytes=64)
+        w_scales = const.tile([P, HALVES, SLOTS], U8, align_bytes=64)
+        nc.vector.memset(w_scales[:].bitcast(I32), 0)
+
+        bias = const.tile([P, SLOTS], BF16)
+        nc.scalar.dma_start(out=bias[:], in_=br.partition_broadcast(P))
+
+        hidden = []
+        for unit in range(UNITS):
+            b, g = divmod(unit, HALVES)
+            h = per_unit.tile([P, PACK, K_PASS], BF16, name="h")
+            nc.sync.dma_start(
+                out=h[:],
+                in_=H[b].rearrange("(p j) d -> p j d", j=PACK)[:, :, g * K_PASS : (g + 1) * K_PASS],
+            )
+            hidden.append(h)
+            if unit == 0:
+                nc.sync.dma_start(
+                    out=w_codes[:].bitcast(I32),
+                    in_=Wr_words.rearrange("g p n t -> p g (n t)").bitcast(I32),
+                )
+                for quad in range(4):
+                    nc.sync.dma_start(
+                        out=w_scales[32 * quad : 32 * quad + 4, :, :].bitcast(I32),
+                        in_=Wr_scales[:, 4 * quad : 4 * quad + 4, :].rearrange("g r n -> r g n").bitcast(I32),
+                    )
+
+        def quantise_along_features(unit):
+            words = hidden[unit][:].bitcast(F32)
+            grouped = per_unit.tile([P, PACK, P, PACK], BF16, name="by_feature", align_bytes=64)
+            for first_j in range(0, PACK, 2):
+                flipped = psum_t.tile([P, 2, 2, P], F32, name="flipped")
+                for j in range(2):
+                    for w in range(2):
+                        nc.tensor.transpose(flipped[:, j, w, :], words[:, first_j + j, w:PAIRS:2], identity[:])
+                nc.scalar.copy(
+                    out=grouped[:, first_j : first_j + 2, :, :].bitcast(F32),
+                    in_=flipped[:].rearrange("p j w f -> p j f w"),
+                )
+            codes = per_unit.tile([P, PACK * P], U32, name="feature_codes", align_bytes=64)
+            scales = per_unit.tile([P, PACK * P], U8, name="feature_scales", align_bytes=64)
+            nc.vector.quantize_mx(
+                out=codes[:].bitcast(FP8X4),
+                scales=scales[:],
+                in_=grouped[:].rearrange("p j f t -> p (j f t)"),
+            )
+            return codes, scales
+
+        def route_of(b, operands):
+            logits = psum_r.tile([P, PACK, SLOTS], F32, name="logits")
+            for j in range(PACK):
+                for g in range(HALVES):
+                    codes, scales = operands[g]
+                    nc.tensor.matmul_mx(
+                        out=logits[:, j, :],
+                        lhsT=codes[:, j * P : (j + 1) * P].bitcast(FP8X4),
+                        lhsT_scale=scales[:, j * P : (j + 1) * P],
+                        rhs=w_codes[:, g, :].bitcast(FP8X4),
+                        rhs_scale=w_scales[:, g, :],
+                        start=(g == 0),
+                        stop=(g == HALVES - 1),
+                    )
+            biased = per_seq.tile([P, SLOTS, PACK], F32, name="biased")
+            nc.vector.tensor_tensor(
+                out=biased[:],
+                in0=logits[:].rearrange("p j s -> p s j"),
+                in1=bias[:].unsqueeze(2).to_broadcast([P, SLOTS, PACK]),
+                op=mybir.AluOpType.add,
+            )
+            route = per_seq.tile([P, SLOTS, PACK], BF16, name="route", align_bytes=64)
+            nc.scalar.activation(out=route[:], in_=biased[:], func=mybir.ActivationFunctionType.Sigmoid)
+            codes = per_seq.tile([P, SLOTS], U32, name="route_codes", align_bytes=64)
+            scales = per_seq.tile([P, SLOTS], U8, name="route_scales", align_bytes=64)
+            nc.vector.quantize_mx(
+                out=codes[:].bitcast(FP8X4),
+                scales=scales[:],
+                in_=route[:].rearrange("p s j -> p (s j)"),
+            )
+            return codes, scales
+
+        routes = []
+        for b in range(SEQS):
+            operands = [quantise_along_features(b * HALVES + g) for g in range(HALVES)]
+            routes.append(route_of(b, operands))
+
+        def regroup(engine_copy, grouped, h, first, count):
+            engine_copy(
+                out=grouped[:, first : first + count, :].rearrange("p (c i) j -> p c j i", i=RUN),
+                in_=h[:, :, first : first + count].rearrange("p j (c i) -> p c j i", i=RUN),
+            )
+
+        for unit in range(UNITS):
+            b, g = divmod(unit, HALVES)
+            grouped = per_unit.tile([P, K_PASS, PACK], BF16, name="by_frame", align_bytes=64)
+            regroup(nc.vector.tensor_copy, grouped, hidden[unit], 0, VECTOR_SHARE)
+            regroup(nc.scalar.copy, grouped, hidden[unit], VECTOR_SHARE, SCALAR_SHARE)
+            codes = per_unit.tile([P, K_PASS], U32, name="frame_codes", align_bytes=64)
+            scales = per_unit.tile([P, K_PASS], U8, name="frame_scales", align_bytes=64)
+            nc.vector.quantize_mx(
+                out=codes[:].bitcast(FP8X4),
+                scales=scales[:],
+                in_=grouped[:].rearrange("p d j -> p (d j)"),
+            )
+            route_codes, route_scales = routes[b]
+            pooled = psum_a.tile([SLOTS, K_PASS], F32, name="pooled")
+            nc.tensor.matmul_mx(
+                out=pooled[:],
+                lhsT=route_codes[:].bitcast(FP8X4),
+                lhsT_scale=route_scales[:],
+                rhs=codes[:].bitcast(FP8X4),
+                rhs_scale=scales[:],
+                start=True,
+                stop=True,
+            )
+            result = per_unit.tile([SLOTS, K_PASS], F32, name="result")
+            nc.scalar.copy(out=result[:], in_=pooled[:])
+            nc.sync.dma_start(out=out[b, :, g * K_PASS : (g + 1) * K_PASS], in_=result[:])

@@ -48,8 +48,15 @@ def tile_instrumentspecificslotmemory_pa_kernel(tc, H, Wr_words, Wr_scales, br, 
         w_scales = const.tile([P, HALVES, SLOTS], U8, align_bytes=64)
         nc.vector.memset(w_scales[:].bitcast(I32), 0)
 
-        bias = const.tile([P, SLOTS], BF16)
-        nc.scalar.dma_start(out=bias[:], in_=br.partition_broadcast(P))
+        bias_row = const.tile([P, SLOTS], BF16)
+        ones = const.tile([P, P], BF16)
+        nc.vector.memset(bias_row[:], 0.0)
+        nc.vector.memset(ones[:], 1.0)
+        nc.scalar.dma_start(out=bias_row[0:1, :], in_=br.unsqueeze(0))
+        spread = psum_r.tile([P, SLOTS], F32, name="spread", tag="logits")
+        nc.tensor.matmul(out=spread[:], lhsT=ones[:], rhs=bias_row[:], start=True, stop=True)
+        bias = const.tile([P, SLOTS], F32)
+        nc.vector.tensor_copy(out=bias[:], in_=spread[:])
 
         hidden = []
         for unit in range(UNITS):
@@ -93,7 +100,7 @@ def tile_instrumentspecificslotmemory_pa_kernel(tc, H, Wr_words, Wr_scales, br, 
             return codes, scales
 
         def route_of(b, operands):
-            logits = psum_r.tile([P, PACK, SLOTS], F32, name="logits")
+            logits = psum_r.tile([P, PACK, SLOTS], F32, name="logits", tag="logits")
             for j in range(PACK):
                 for g in range(HALVES):
                     codes, scales = operands[g]

@@ -23,6 +23,8 @@ SCALAR_SHARE = K_PASS // 4
 VECTOR_SHARE = K_PASS - SCALAR_SHARE
 RUN = 4
 
+W_BEHIND_UNIT = 2
+
 FLOPS = 2 * (2 * SEQS * FRAMES * FEATURES * SLOTS)
 
 
@@ -67,7 +69,7 @@ def tile_instrumentspecificslotmemory_pa_kernel(tc, H, Wr_words, Wr_scales, br, 
                 in_=H[b].rearrange("(p j) d -> p j d", j=PACK)[:, :, g * K_PASS : (g + 1) * K_PASS],
             )
             hidden.append(h)
-            if unit == 0:
+            if unit == W_BEHIND_UNIT:
                 nc.sync.dma_start(
                     out=w_codes[:].bitcast(I32),
                     in_=Wr_words.rearrange("g p n t -> p g (n t)").bitcast(I32),

@@ -19,11 +19,9 @@ HALVES = FEATURES // K_PASS
 UNITS = SEQS * HALVES
 PAIRS = K_PASS // 2
 
-SCALAR_SHARE = K_PASS // 4
+SCALAR_SHARE = 96
 VECTOR_SHARE = K_PASS - SCALAR_SHARE
 RUN = 4
-
-W_BEHIND_UNIT = 2
 
 FLOPS = 2 * (2 * SEQS * FRAMES * FEATURES * SLOTS)
 
@@ -69,7 +67,7 @@ def tile_instrumentspecificslotmemory_pa_kernel(tc, H, Wr_words, Wr_scales, br, 
                 in_=H[b].rearrange("(p j) d -> p j d", j=PACK)[:, :, g * K_PASS : (g + 1) * K_PASS],
             )
             hidden.append(h)
-            if unit == W_BEHIND_UNIT:
+            if unit == 0:
                 nc.sync.dma_start(
                     out=w_codes[:].bitcast(I32),
                     in_=Wr_words.rearrange("g p n t -> p g (n t)").bitcast(I32),

@@ -19,9 +19,11 @@ HALVES = FEATURES // K_PASS
 UNITS = SEQS * HALVES
 PAIRS = K_PASS // 2
 
-SCALAR_SHARE = 96
+SCALAR_SHARE = 80
 VECTOR_SHARE = K_PASS - SCALAR_SHARE
 RUN = 4
+
+BIAS_COPIES = 8
 
 FLOPS = 2 * (2 * SEQS * FRAMES * FEATURES * SLOTS)
 
@@ -33,8 +35,10 @@ def tile_instrumentspecificslotmemory_pa_kernel(tc, H, Wr_words, Wr_scales, br, 
         per_unit = ctx.enter_context(tc.tile_pool(name="per_unit", bufs=UNITS))
         per_seq = ctx.enter_context(tc.tile_pool(name="per_seq", bufs=SEQS))
         psum_t = ctx.enter_context(tc.psum_pool(name="psum_t", bufs=4))
-        psum_r = ctx.enter_context(tc.psum_pool(name="psum_r", bufs=2))
+        psum_r = ctx.enter_context(tc.psum_pool(name="psum_r", bufs=1))
         psum_a = ctx.enter_context(tc.psum_pool(name="psum_a", bufs=2))
+
+        ctx.enter_context(tc.manual_schedule())
 
         identity = const.tile([P, P], F32)
         make_identity(nc, identity[:])
@@ -49,14 +53,16 @@ def tile_instrumentspecificslotmemory_pa_kernel(tc, H, Wr_words, Wr_scales, br, 
         nc.vector.memset(w_scales[:].bitcast(I32), 0)
 
         bias_row = const.tile([P, SLOTS], BF16)
-        ones = const.tile([P, P], BF16)
+        ones = const.tile([P, BIAS_COPIES], BF16)
         nc.vector.memset(bias_row[:], 0.0)
         nc.vector.memset(ones[:], 1.0)
         nc.scalar.dma_start(out=bias_row[0:1, :], in_=br.unsqueeze(0))
-        spread = psum_r.tile([P, SLOTS], F32, name="spread", tag="logits")
-        nc.tensor.matmul(out=spread[:], lhsT=ones[:], rhs=bias_row[:], start=True, stop=True)
-        bias = const.tile([P, SLOTS], F32)
-        nc.vector.tensor_copy(out=bias[:], in_=spread[:])
+        turned = psum_r.tile([SLOTS, BIAS_COPIES], F32, name="bias_turned", tag="turned")
+        bias = const.tile([SLOTS, BIAS_COPIES], F32)
+
+        def turn_bias():
+            nc.tensor.matmul(out=turned[:], lhsT=bias_row[:], rhs=ones[:], start=True, stop=True)
+            nc.vector.tensor_copy(out=bias[:], in_=turned[:])
 
         hidden = []
         for unit in range(UNITS):
@@ -78,7 +84,9 @@ def tile_instrumentspecificslotmemory_pa_kernel(tc, H, Wr_words, Wr_scales, br, 
                         in_=Wr_scales[:, 4 * quad : 4 * quad + 4, :].rearrange("g r n -> r g n").bitcast(I32),
                     )
 
-        def quantise_along_features(unit):
+        by_feature, feature_operands = [], []
+
+        def turn_unit(unit):
             words = hidden[unit][:].bitcast(F32)
             grouped = per_unit.tile([P, PACK, P, PACK], BF16, name="by_feature", align_bytes=64)
             for first_j in range(0, PACK, 2):
@@ -90,51 +98,71 @@ def tile_instrumentspecificslotmemory_pa_kernel(tc, H, Wr_words, Wr_scales, br, 
                     out=grouped[:, first_j : first_j + 2, :, :].bitcast(F32),
                     in_=flipped[:].rearrange("p j w f -> p j f w"),
                 )
+            by_feature.append(grouped)
+
+        def quantise_along_features(unit):
             codes = per_unit.tile([P, PACK * P], U32, name="feature_codes", align_bytes=64)
             scales = per_unit.tile([P, PACK * P], U8, name="feature_scales", align_bytes=64)
             nc.vector.quantize_mx(
                 out=codes[:].bitcast(FP8X4),
                 scales=scales[:],
-                in_=grouped[:].rearrange("p j f t -> p (j f t)"),
+                in_=by_feature[unit][:].rearrange("p j f t -> p (j f t)"),
             )
-            return codes, scales
+            feature_operands.append((codes, scales))
 
-        def route_of(b, operands):
-            logits = psum_r.tile([P, PACK, SLOTS], F32, name="logits", tag="logits")
-            for j in range(PACK):
-                for g in range(HALVES):
-                    codes, scales = operands[g]
-                    nc.tensor.matmul_mx(
-                        out=logits[:, j, :],
-                        lhsT=codes[:, j * P : (j + 1) * P].bitcast(FP8X4),
-                        lhsT_scale=scales[:, j * P : (j + 1) * P],
-                        rhs=w_codes[:, g, :].bitcast(FP8X4),
-                        rhs_scale=w_scales[:, g, :],
-                        start=(g == 0),
-                        stop=(g == HALVES - 1),
-                    )
-            biased = per_seq.tile([P, SLOTS, PACK], F32, name="biased")
-            nc.vector.tensor_tensor(
-                out=biased[:],
-                in0=logits[:].rearrange("p j s -> p s j"),
-                in1=bias[:].unsqueeze(2).to_broadcast([P, SLOTS, PACK]),
-                op=mybir.AluOpType.add,
+        logits_of, by_slot_of, turned_of, route_of, route_operands = [], [], [], [], []
+
+        def multiply_by_w(b):
+            logits = psum_r.tile([SLOTS, PACK, P], F32, name="logits")
+            for g in range(HALVES):
+                codes, scales = feature_operands[b * HALVES + g]
+                nc.tensor.matmul_mx(
+                    out=logits[:].rearrange("s j p -> s (j p)"),
+                    lhsT=w_codes[:, g, :].bitcast(FP8X4),
+                    lhsT_scale=w_scales[:, g, :],
+                    rhs=codes[:].bitcast(FP8X4),
+                    rhs_scale=scales[:],
+                    start=(g == 0),
+                    stop=(g == HALVES - 1),
+                )
+            logits_of.append(logits)
+
+        def sigmoid(b):
+            by_slot = per_seq.tile([SLOTS, P, PACK], BF16, name="by_slot")
+            nc.scalar.activation(
+                out=by_slot[:],
+                in_=logits_of[b][:].rearrange("s j p -> s p j"),
+                func=mybir.ActivationFunctionType.Sigmoid,
+                bias=bias[:, 0:1],
             )
+            by_slot_of.append(by_slot)
+
+        def turn_route(b):
+            words = by_slot_of[b][:].rearrange("s p j -> s (p j)").bitcast(F32)
+            turned = psum_r.tile([P, 2, SLOTS], F32, name="turned", tag="turned")
+            for u in range(2):
+                nc.tensor.transpose(turned[:, u, :], words[:, u : 2 * P : 2], identity[:])
+            turned_of.append(turned)
+
+        def fetch_route(b):
             route = per_seq.tile([P, SLOTS, PACK], BF16, name="route", align_bytes=64)
-            nc.scalar.activation(out=route[:], in_=biased[:], func=mybir.ActivationFunctionType.Sigmoid)
+            nc.vector.tensor_copy(
+                out=route[:].rearrange("p s j -> p (s j)").bitcast(F32).rearrange("p (s u) -> p s u", u=2),
+                in_=turned_of[b][:].rearrange("p u s -> p s u"),
+            )
+            route_of.append(route)
+
+        def quantise_route(b):
             codes = per_seq.tile([P, SLOTS], U32, name="route_codes", align_bytes=64)
             scales = per_seq.tile([P, SLOTS], U8, name="route_scales", align_bytes=64)
             nc.vector.quantize_mx(
                 out=codes[:].bitcast(FP8X4),
                 scales=scales[:],
-                in_=route[:].rearrange("p s j -> p (s j)"),
+                in_=route_of[b][:].rearrange("p s j -> p (s j)"),
             )
-            return codes, scales
+            route_operands.append((codes, scales))
 
-        routes = []
-        for b in range(SEQS):
-            operands = [quantise_along_features(b * HALVES + g) for g in range(HALVES)]
-            routes.append(route_of(b, operands))
+        by_frame, frame_operands = [], []
 
         def regroup(engine_copy, grouped, h, first, count):
             engine_copy(
@@ -142,29 +170,79 @@ def tile_instrumentspecificslotmemory_pa_kernel(tc, H, Wr_words, Wr_scales, br, 
                 in_=h[:, :, first : first + count].rearrange("p j (c i) -> p c j i", i=RUN),
             )
 
-        for unit in range(UNITS):
-            b, g = divmod(unit, HALVES)
+        def regroup_unit(unit):
             grouped = per_unit.tile([P, K_PASS, PACK], BF16, name="by_frame", align_bytes=64)
             regroup(nc.vector.tensor_copy, grouped, hidden[unit], 0, VECTOR_SHARE)
             regroup(nc.scalar.copy, grouped, hidden[unit], VECTOR_SHARE, SCALAR_SHARE)
+            by_frame.append(grouped)
+
+        def quantise_along_frames(unit):
             codes = per_unit.tile([P, K_PASS], U32, name="frame_codes", align_bytes=64)
             scales = per_unit.tile([P, K_PASS], U8, name="frame_scales", align_bytes=64)
             nc.vector.quantize_mx(
                 out=codes[:].bitcast(FP8X4),
                 scales=scales[:],
-                in_=grouped[:].rearrange("p d j -> p (d j)"),
+                in_=by_frame[unit][:].rearrange("p d j -> p (d j)"),
             )
-            route_codes, route_scales = routes[b]
+            frame_operands.append((codes, scales))
+
+        def pool(unit, engine_copy, first=0, count=K_PASS):
+            b, g = divmod(unit, HALVES)
+            columns = slice(first, first + count)
+            route_codes, route_scales = route_operands[b]
+            codes, scales = frame_operands[unit]
             pooled = psum_a.tile([SLOTS, K_PASS], F32, name="pooled")
             nc.tensor.matmul_mx(
-                out=pooled[:],
+                out=pooled[:, :count],
                 lhsT=route_codes[:].bitcast(FP8X4),
                 lhsT_scale=route_scales[:],
-                rhs=codes[:].bitcast(FP8X4),
-                rhs_scale=scales[:],
+                rhs=codes[:, columns].bitcast(FP8X4),
+                rhs_scale=scales[:, columns],
                 start=True,
                 stop=True,
             )
             result = per_unit.tile([SLOTS, K_PASS], F32, name="result")
-            nc.scalar.copy(out=result[:], in_=pooled[:])
-            nc.sync.dma_start(out=out[b, :, g * K_PASS : (g + 1) * K_PASS], in_=result[:])
+            engine_copy(out=result[:, :count], in_=pooled[:, :count])
+            nc.sync.dma_start(out=out[b, :, g * K_PASS + first : g * K_PASS + first + count], in_=result[:, :count])
+
+        regroup_unit(0)
+        regroup_unit(1)
+        turn_unit(0)
+        quantise_along_frames(0)
+        regroup_unit(2)
+        turn_unit(1)
+        turn_bias()
+        quantise_along_features(0)
+        for b in range(SEQS):
+            last = b == SEQS - 1
+            quantise_along_features(2 * b + 1)
+            if not last:
+                turn_unit(2 * b + 2)
+            if b > 0:
+                turn_route(b - 1)
+                fetch_route(b - 1)
+            multiply_by_w(b)
+            quantise_along_frames(b + 1)
+            if b > 0:
+                quantise_route(b - 1)
+            if not last:
+                quantise_along_features(2 * b + 2)
+                turn_unit(2 * b + 3)
+            sigmoid(b)
+            if b >= 2:
+                pool(2 * b - 4, nc.scalar.copy)
+                pool(2 * b - 3, nc.scalar.copy)
+            regroup_unit(b + 3)
+
+        turn_route(SEQS - 1)
+        fetch_route(SEQS - 1)
+        quantise_along_frames(5)
+        quantise_route(SEQS - 1)
+        pool(4, nc.scalar.copy)
+        pool(5, nc.scalar.copy)
+        regroup_unit(7)
+        quantise_along_frames(6)
+        pool(6, nc.scalar.copy)
+        quantise_along_frames(7)
+        pool(7, nc.scalar.copy, 0, K_PASS // 2)
+        pool(7, nc.vector.tensor_copy, K_PASS // 2, K_PASS // 2)

@@ -53,15 +53,34 @@ def tile_instrumentspecificslotmemory_pa_kernel(tc, H, Wr_words, Wr_scales, br, 
         nc.vector.memset(w_scales[:].bitcast(I32), 0)
 
         bias_row = const.tile([P, SLOTS], BF16)
-        ones = const.tile([P, BIAS_COPIES], BF16)
-        nc.vector.memset(bias_row[:], 0.0)
+        ones = const.tile([P, K_PASS], BF16)
         nc.vector.memset(ones[:], 1.0)
+        nc.vector.memset(bias_row[:], 0.0)
         nc.scalar.dma_start(out=bias_row[0:1, :], in_=br.unsqueeze(0))
         turned = psum_r.tile([SLOTS, BIAS_COPIES], F32, name="bias_turned", tag="turned")
         bias = const.tile([SLOTS, BIAS_COPIES], F32)
 
+        def keep_warm(count):
+            for i in range(count):
+                unused = psum_a.tile([P, K_PASS], F32, name="unused", tag="pooled")
+                nc.tensor.matmul(out=unused[:], lhsT=ones[:, :P], rhs=ones[:], start=True, stop=True)
+
+        def keep_warm_mx(count):
+            w_columns = HALVES * SLOTS
+            for i in range(count):
+                unused = psum_a.tile([P, K_PASS], F32, name="unused", tag="pooled")
+                nc.tensor.matmul_mx(
+                    out=unused[:, :w_columns],
+                    lhsT=w_codes[:, 0, :].bitcast(FP8X4),
+                    lhsT_scale=w_scales[:, 0, :],
+                    rhs=w_codes[:].rearrange("p g n -> p (g n)").bitcast(FP8X4),
+                    rhs_scale=w_scales[:].rearrange("p g n -> p (g n)"),
+                    start=True,
+                    stop=True,
+                )
+
         def turn_bias():
-            nc.tensor.matmul(out=turned[:], lhsT=bias_row[:], rhs=ones[:], start=True, stop=True)
+            nc.tensor.matmul(out=turned[:], lhsT=bias_row[:], rhs=ones[:, :BIAS_COPIES], start=True, stop=True)
             nc.vector.tensor_copy(out=bias[:], in_=turned[:])
 
         hidden = []
@@ -186,12 +205,14 @@ def tile_instrumentspecificslotmemory_pa_kernel(tc, H, Wr_words, Wr_scales, br, 
             )
             frame_operands.append((codes, scales))
 
-        def pool(unit, engine_copy, first=0, count=K_PASS):
+        def pool(unit, engine_copy, first=0, count=K_PASS, bank=None):
             b, g = divmod(unit, HALVES)
             columns = slice(first, first + count)
             route_codes, route_scales = route_operands[b]
             codes, scales = frame_operands[unit]
-            pooled = psum_a.tile([SLOTS, K_PASS], F32, name="pooled")
+            if bank is None:
+                bank = psum_a.tile([SLOTS, K_PASS], F32, name="pooled")
+            pooled = bank
             nc.tensor.matmul_mx(
                 out=pooled[:, :count],
                 lhsT=route_codes[:].bitcast(FP8X4),
@@ -205,13 +226,16 @@ def tile_instrumentspecificslotmemory_pa_kernel(tc, H, Wr_words, Wr_scales, br, 
             engine_copy(out=result[:, :count], in_=pooled[:, :count])
             nc.sync.dma_start(out=out[b, :, g * K_PASS + first : g * K_PASS + first + count], in_=result[:, :count])
 
+        keep_warm(5)
         regroup_unit(0)
         regroup_unit(1)
         turn_unit(0)
+        turn_bias()
+        keep_warm(1)
         quantise_along_frames(0)
         regroup_unit(2)
         turn_unit(1)
-        turn_bias()
+        keep_warm_mx(4)
         quantise_along_features(0)
         for b in range(SEQS):
             last = b == SEQS - 1
@@ -245,4 +269,5 @@ def tile_instrumentspecificslotmemory_pa_kernel(tc, H, Wr_words, Wr_scales, br, 
         pool(6, nc.scalar.copy)
         quantise_along_frames(7)
         pool(7, nc.scalar.copy, 0, K_PASS // 2)
-        pool(7, nc.vector.tensor_copy, K_PASS // 2, K_PASS // 2)
+        second = psum_r.tile([SLOTS, K_PASS], F32, name="second", tag="logits")
+        pool(7, nc.vector.tensor_copy, K_PASS // 2, K_PASS // 2, second)

@@ -252,6 +252,8 @@ def tile_instrumentspecificslotmemory_pa_kernel(tc, H, Wr_words, Wr_scales, br, 
             if not last:
                 quantise_along_features(2 * b + 2)
                 turn_unit(2 * b + 3)
+                if b < 2:
+                    keep_warm_mx(4)
             sigmoid(b)
             if b >= 2:
                 pool(2 * b - 4, nc.scalar.copy)

@@ -19,8 +19,7 @@ HALVES = FEATURES // K_PASS
 UNITS = SEQS * HALVES
 PAIRS = K_PASS // 2
 
-SCALAR_SHARE = 80
-VECTOR_SHARE = K_PASS - SCALAR_SHARE
+SCALAR_SHARE = [128] + 5 * [48] + 2 * [96]
 RUN = 4
 
 BIAS_COPIES = 8
@@ -87,12 +86,16 @@ def tile_instrumentspecificslotmemory_pa_kernel(tc, H, Wr_words, Wr_scales, br, 
         for unit in range(UNITS):
             b, g = divmod(unit, HALVES)
             h = per_unit.tile([P, PACK, K_PASS], BF16, name="h")
-            nc.sync.dma_start(
-                out=h[:],
-                in_=H[b].rearrange("(p j) d -> p j d", j=PACK)[:, :, g * K_PASS : (g + 1) * K_PASS],
-            )
+            piece = K_PASS // 2 if unit == 0 else K_PASS
+            for first in range(0, K_PASS, piece):
+                nc.sync.dma_start(
+                    out=h[:, :, first : first + piece],
+                    in_=H[b].rearrange("(p j) d -> p j d", j=PACK)[
+                        :, :, g * K_PASS + first : g * K_PASS + first + piece
+                    ],
+                )
             hidden.append(h)
-            if unit == 0:
+            if unit == 1:
                 nc.sync.dma_start(
                     out=w_codes[:].bitcast(I32),
                     in_=Wr_words.rearrange("g p n t -> p g (n t)").bitcast(I32),
@@ -165,7 +168,7 @@ def tile_instrumentspecificslotmemory_pa_kernel(tc, H, Wr_words, Wr_scales, br, 
 
         def fetch_route(b):
             route = per_seq.tile([P, SLOTS, PACK], BF16, name="route", align_bytes=64)
-            nc.vector.tensor_copy(
+            nc.scalar.copy(
                 out=route[:].rearrange("p s j -> p (s j)").bitcast(F32).rearrange("p (s u) -> p s u", u=2),
                 in_=turned_of[b][:].rearrange("p u s -> p s u"),
             )
@@ -189,20 +192,28 @@ def tile_instrumentspecificslotmemory_pa_kernel(tc, H, Wr_words, Wr_scales, br, 
                 in_=h[:, :, first : first + count].rearrange("p j (c i) -> p c j i", i=RUN),
             )
 
-        def regroup_unit(unit):
+        def regroup_on_vector(unit):
             grouped = per_unit.tile([P, K_PASS, PACK], BF16, name="by_frame", align_bytes=64)
-            regroup(nc.vector.tensor_copy, grouped, hidden[unit], 0, VECTOR_SHARE)
-            regroup(nc.scalar.copy, grouped, hidden[unit], VECTOR_SHARE, SCALAR_SHARE)
+            share = K_PASS - SCALAR_SHARE[unit]
+            piece = K_PASS // 2 if unit == 0 else share
+            for first in range(0, share, piece):
+                regroup(nc.vector.tensor_copy, grouped, hidden[unit], first, min(piece, share - first))
             by_frame.append(grouped)
 
-        def quantise_along_frames(unit):
+        def regroup_on_scalar(unit):
+            share = SCALAR_SHARE[unit]
+            regroup(nc.scalar.copy, by_frame[unit], hidden[unit], K_PASS - share, share)
+
+        def quantise_along_frames(unit, pieces=1):
             codes = per_unit.tile([P, K_PASS], U32, name="frame_codes", align_bytes=64)
             scales = per_unit.tile([P, K_PASS], U8, name="frame_scales", align_bytes=64)
-            nc.vector.quantize_mx(
-                out=codes[:].bitcast(FP8X4),
-                scales=scales[:],
-                in_=by_frame[unit][:].rearrange("p d j -> p (d j)"),
-            )
+            width = K_PASS // pieces
+            for first in range(0, K_PASS, width):
+                nc.vector.quantize_mx(
+                    out=codes[:, first : first + width].bitcast(FP8X4),
+                    scales=scales[:, first : first + width],
+                    in_=by_frame[unit][:, first : first + width, :].rearrange("p d j -> p (d j)"),
+                )
             frame_operands.append((codes, scales))
 
         def pool(unit, engine_copy, first=0, count=K_PASS, bank=None):
@@ -226,50 +237,61 @@ def tile_instrumentspecificslotmemory_pa_kernel(tc, H, Wr_words, Wr_scales, br, 
             engine_copy(out=result[:, :count], in_=pooled[:, :count])
             nc.sync.dma_start(out=out[b, :, g * K_PASS + first : g * K_PASS + first + count], in_=result[:, :count])
 
-        keep_warm(5)
-        regroup_unit(0)
-        regroup_unit(1)
+        keep_warm(4)
+        regroup_on_vector(0)
+        regroup_on_scalar(0)
         turn_unit(0)
+        regroup_on_vector(1)
+        turn_unit(1)
+        regroup_on_scalar(1)
         turn_bias()
         keep_warm(1)
-        quantise_along_frames(0)
-        regroup_unit(2)
-        turn_unit(1)
-        keep_warm_mx(4)
-        quantise_along_features(0)
         for b in range(SEQS):
-            last = b == SEQS - 1
+            quantise_along_features(2 * b)
+            quantise_along_frames(b)
             quantise_along_features(2 * b + 1)
-            if not last:
-                turn_unit(2 * b + 2)
-            if b > 0:
-                turn_route(b - 1)
-                fetch_route(b - 1)
-            multiply_by_w(b)
-            quantise_along_frames(b + 1)
-            if b > 0:
-                quantise_route(b - 1)
-            if not last:
-                quantise_along_features(2 * b + 2)
-                turn_unit(2 * b + 3)
-                if b < 2:
-                    keep_warm_mx(4)
-            sigmoid(b)
             if b >= 2:
-                pool(2 * b - 4, nc.scalar.copy)
-                pool(2 * b - 3, nc.scalar.copy)
-            regroup_unit(b + 3)
+                fetch_route(b - 2)
+                quantise_route(b - 2)
+            if b >= 1:
+                sigmoid(b - 1)
+            if b < SEQS - 1:
+                turn_unit(2 * b + 2)
+                if b == 0:
+                    keep_warm(1)
+                else:
+                    keep_warm_mx(4)
+                regroup_on_vector(b + 2)
+                regroup_on_scalar(b + 2)
+                turn_unit(2 * b + 3)
+            else:
+                pool(0, nc.scalar.copy)
+                pool(1, nc.scalar.copy)
+                regroup_on_vector(5)
+                regroup_on_scalar(5)
+            if b >= 1:
+                turn_route(b - 1)
+            multiply_by_w(b)
 
-        turn_route(SEQS - 1)
-        fetch_route(SEQS - 1)
+        quantise_along_frames(4)
+        fetch_route(2)
+        sigmoid(3)
+        regroup_on_vector(6)
+        regroup_on_scalar(6)
+        quantise_route(2)
+        pool(2, nc.scalar.copy)
+        pool(3, nc.scalar.copy)
         quantise_along_frames(5)
-        quantise_route(SEQS - 1)
+        turn_route(3)
+        fetch_route(3)
+        regroup_on_vector(7)
+        regroup_on_scalar(7)
+        quantise_route(3)
         pool(4, nc.scalar.copy)
         pool(5, nc.scalar.copy)
-        regroup_unit(7)
         quantise_along_frames(6)
         pool(6, nc.scalar.copy)
-        quantise_along_frames(7)
+        quantise_along_frames(7, pieces=2)
         pool(7, nc.scalar.copy, 0, K_PASS // 2)
         second = psum_r.tile([SLOTS, K_PASS], F32, name="second", tag="logits")
         pool(7, nc.vector.tensor_copy, K_PASS // 2, K_PASS // 2, second)

@@ -64,10 +64,10 @@ def tile_instrumentspecificslotmemory_pa_kernel(tc, H, Wr_words, Wr_scales, br, 
                 unused = psum_a.tile([P, K_PASS], F32, name="unused", tag="pooled")
                 nc.tensor.matmul(out=unused[:], lhsT=ones[:, :P], rhs=ones[:], start=True, stop=True)
 
-        def keep_warm_mx(count):
+        def keep_warm_mx(count, banks=psum_a, tag="pooled"):
             w_columns = HALVES * SLOTS
             for i in range(count):
-                unused = psum_a.tile([P, K_PASS], F32, name="unused", tag="pooled")
+                unused = banks.tile([P, K_PASS], F32, name="unused", tag=tag)
                 nc.tensor.matmul_mx(
                     out=unused[:, :w_columns],
                     lhsT=w_codes[:, 0, :].bitcast(FP8X4),
@@ -150,20 +150,20 @@ def tile_instrumentspecificslotmemory_pa_kernel(tc, H, Wr_words, Wr_scales, br, 
             logits_of.append(logits)
 
         def sigmoid(b):
-            by_slot = per_seq.tile([SLOTS, P, PACK], BF16, name="by_slot")
+            by_slot = per_seq.tile([SLOTS, 2, P, 2], BF16, name="by_slot")
             nc.scalar.activation(
                 out=by_slot[:],
-                in_=logits_of[b][:].rearrange("s j p -> s p j"),
+                in_=logits_of[b][:].rearrange("s (u e) p -> s u p e", u=2),
                 func=mybir.ActivationFunctionType.Sigmoid,
                 bias=bias[:, 0:1],
             )
             by_slot_of.append(by_slot)
 
         def turn_route(b):
-            words = by_slot_of[b][:].rearrange("s p j -> s (p j)").bitcast(F32)
+            words = by_slot_of[b][:].rearrange("s u p e -> s (u p e)").bitcast(F32)
             turned = psum_r.tile([P, 2, SLOTS], F32, name="turned", tag="turned")
             for u in range(2):
-                nc.tensor.transpose(turned[:, u, :], words[:, u : 2 * P : 2], identity[:])
+                nc.tensor.transpose(turned[:, u, :], words[:, u * P : (u + 1) * P], identity[:])
             turned_of.append(turned)
 
         def fetch_route(b):
@@ -241,6 +241,7 @@ def tile_instrumentspecificslotmemory_pa_kernel(tc, H, Wr_words, Wr_scales, br, 
         regroup_on_vector(0)
         regroup_on_scalar(0)
         turn_unit(0)
+        keep_warm(1)
         regroup_on_vector(1)
         turn_unit(1)
         regroup_on_scalar(1)
@@ -257,10 +258,7 @@ def tile_instrumentspecificslotmemory_pa_kernel(tc, H, Wr_words, Wr_scales, br, 
                 sigmoid(b - 1)
             if b < SEQS - 1:
                 turn_unit(2 * b + 2)
-                if b == 0:
-                    keep_warm(1)
-                else:
-                    keep_warm_mx(4)
+                keep_warm_mx(2 if b == 0 else 4)
                 regroup_on_vector(b + 2)
                 regroup_on_scalar(b + 2)
                 turn_unit(2 * b + 3)
@@ -283,12 +281,14 @@ def tile_instrumentspecificslotmemory_pa_kernel(tc, H, Wr_words, Wr_scales, br, 
         pool(3, nc.scalar.copy)
         quantise_along_frames(5)
         turn_route(3)
+        keep_warm_mx(2, psum_t, "flipped")
         fetch_route(3)
         regroup_on_vector(7)
         regroup_on_scalar(7)
         quantise_route(3)
         pool(4, nc.scalar.copy)
         pool(5, nc.scalar.copy)
+        keep_warm_mx(2, psum_t, "flipped")
         quantise_along_frames(6)
         pool(6, nc.scalar.copy)
         quantise_along_frames(7, pieces=2)

@@ -34,8 +34,8 @@ def tile_instrumentspecificslotmemory_pa_kernel(tc, H, Wr_words, Wr_scales, br, 
         per_unit = ctx.enter_context(tc.tile_pool(name="per_unit", bufs=UNITS))
         per_seq = ctx.enter_context(tc.tile_pool(name="per_seq", bufs=SEQS))
         psum_t = ctx.enter_context(tc.psum_pool(name="psum_t", bufs=4))
+        psum_l = ctx.enter_context(tc.psum_pool(name="psum_l", bufs=2))
         psum_r = ctx.enter_context(tc.psum_pool(name="psum_r", bufs=1))
-        psum_a = ctx.enter_context(tc.psum_pool(name="psum_a", bufs=2))
 
         ctx.enter_context(tc.manual_schedule())
 
@@ -52,22 +52,24 @@ def tile_instrumentspecificslotmemory_pa_kernel(tc, H, Wr_words, Wr_scales, br, 
         nc.vector.memset(w_scales[:].bitcast(I32), 0)
 
         bias_row = const.tile([P, SLOTS], BF16)
-        ones = const.tile([P, K_PASS], BF16)
+        ones = const.tile([P, P], BF16)
         nc.vector.memset(ones[:], 1.0)
         nc.vector.memset(bias_row[:], 0.0)
         nc.scalar.dma_start(out=bias_row[0:1, :], in_=br.unsqueeze(0))
         turned = psum_r.tile([SLOTS, BIAS_COPIES], F32, name="bias_turned", tag="turned")
         bias = const.tile([SLOTS, BIAS_COPIES], F32)
 
-        def keep_warm(count):
-            for i in range(count):
-                unused = psum_a.tile([P, K_PASS], F32, name="unused", tag="pooled")
-                nc.tensor.matmul(out=unused[:], lhsT=ones[:, :P], rhs=ones[:], start=True, stop=True)
-
-        def keep_warm_mx(count, banks=psum_a, tag="pooled"):
-            w_columns = HALVES * SLOTS
+        def keep_warm(count, banks=psum_r, tag="unused"):
             for i in range(count):
                 unused = banks.tile([P, K_PASS], F32, name="unused", tag=tag)
+                nc.tensor.matmul(
+                    out=unused[:], lhsT=ones[:], rhs=ones[:, 0:1].to_broadcast([P, K_PASS]), start=True, stop=True
+                )
+
+        def keep_warm_mx(count):
+            w_columns = HALVES * SLOTS
+            for i in range(count):
+                unused = psum_r.tile([P, K_PASS], F32, name="unused")
                 nc.tensor.matmul_mx(
                     out=unused[:, :w_columns],
                     lhsT=w_codes[:, 0, :].bitcast(FP8X4),
@@ -134,20 +136,20 @@ def tile_instrumentspecificslotmemory_pa_kernel(tc, H, Wr_words, Wr_scales, br, 
 
         logits_of, by_slot_of, turned_of, route_of, route_operands = [], [], [], [], []
 
-        def multiply_by_w(b):
-            logits = psum_r.tile([SLOTS, PACK, P], F32, name="logits")
-            for g in range(HALVES):
-                codes, scales = feature_operands[b * HALVES + g]
-                nc.tensor.matmul_mx(
-                    out=logits[:].rearrange("s j p -> s (j p)"),
-                    lhsT=w_codes[:, g, :].bitcast(FP8X4),
-                    lhsT_scale=w_scales[:, g, :],
-                    rhs=codes[:].bitcast(FP8X4),
-                    rhs_scale=scales[:],
-                    start=(g == 0),
-                    stop=(g == HALVES - 1),
-                )
-            logits_of.append(logits)
+        def multiply_by_w(b, g):
+            if g == 0:
+                logits = psum_l.tile([SLOTS, PACK, P], F32, name="logits")
+                logits_of.append(logits)
+            codes, scales = feature_operands[b * HALVES + g]
+            nc.tensor.matmul_mx(
+                out=logits_of[b][:].rearrange("s j p -> s (j p)"),
+                lhsT=w_codes[:, g, :].bitcast(FP8X4),
+                lhsT_scale=w_scales[:, g, :],
+                rhs=codes[:].bitcast(FP8X4),
+                rhs_scale=scales[:],
+                start=(g == 0),
+                stop=(g == HALVES - 1),
+            )
 
         def sigmoid(b):
             by_slot = per_seq.tile([SLOTS, 2, P, 2], BF16, name="by_slot")
@@ -216,14 +218,12 @@ def tile_instrumentspecificslotmemory_pa_kernel(tc, H, Wr_words, Wr_scales, br, 
                 )
             frame_operands.append((codes, scales))
 
-        def pool(unit, engine_copy, first=0, count=K_PASS, bank=None):
+        def pool(unit, engine_copy, first=0, count=K_PASS):
             b, g = divmod(unit, HALVES)
             columns = slice(first, first + count)
             route_codes, route_scales = route_operands[b]
             codes, scales = frame_operands[unit]
-            if bank is None:
-                bank = psum_a.tile([SLOTS, K_PASS], F32, name="pooled")
-            pooled = bank
+            pooled = psum_t.tile([SLOTS, K_PASS], F32, name="pooled", tag="flipped")
             nc.tensor.matmul_mx(
                 out=pooled[:, :count],
                 lhsT=route_codes[:].bitcast(FP8X4),
@@ -237,7 +237,7 @@ def tile_instrumentspecificslotmemory_pa_kernel(tc, H, Wr_words, Wr_scales, br, 
             engine_copy(out=result[:, :count], in_=pooled[:, :count])
             nc.sync.dma_start(out=out[b, :, g * K_PASS + first : g * K_PASS + first + count], in_=result[:, :count])
 
-        keep_warm(4)
+        keep_warm(4, psum_t, "flipped")
         regroup_on_vector(0)
         regroup_on_scalar(0)
         turn_unit(0)
@@ -258,18 +258,23 @@ def tile_instrumentspecificslotmemory_pa_kernel(tc, H, Wr_words, Wr_scales, br, 
                 sigmoid(b - 1)
             if b < SEQS - 1:
                 turn_unit(2 * b + 2)
-                keep_warm_mx(2 if b == 0 else 4)
+                multiply_by_w(b, 0)
+                if b >= 1:
+                    keep_warm_mx(1)
                 regroup_on_vector(b + 2)
                 regroup_on_scalar(b + 2)
                 turn_unit(2 * b + 3)
             else:
                 pool(0, nc.scalar.copy)
+                multiply_by_w(b, 0)
                 pool(1, nc.scalar.copy)
                 regroup_on_vector(5)
                 regroup_on_scalar(5)
             if b >= 1:
                 turn_route(b - 1)
-            multiply_by_w(b)
+            multiply_by_w(b, 1)
+            if b < SEQS - 1:
+                keep_warm_mx(1)
 
         quantise_along_frames(4)
         fetch_route(2)
@@ -281,17 +286,16 @@ def tile_instrumentspecificslotmemory_pa_kernel(tc, H, Wr_words, Wr_scales, br, 
         pool(3, nc.scalar.copy)
         quantise_along_frames(5)
         turn_route(3)
-        keep_warm_mx(2, psum_t, "flipped")
+        keep_warm_mx(2)
         fetch_route(3)
         regroup_on_vector(7)
         regroup_on_scalar(7)
         quantise_route(3)
         pool(4, nc.scalar.copy)
         pool(5, nc.scalar.copy)
-        keep_warm_mx(2, psum_t, "flipped")
+        keep_warm_mx(2)
         quantise_along_frames(6)
         pool(6, nc.scalar.copy)
         quantise_along_frames(7, pieces=2)
         pool(7, nc.scalar.copy, 0, K_PASS // 2)
-        second = psum_r.tile([SLOTS, K_PASS], F32, name="second", tag="logits")
-        pool(7, nc.vector.tensor_copy, K_PASS // 2, K_PASS // 2, second)
+        pool(7, nc.vector.tensor_copy, K_PASS // 2, K_PASS // 2)

from contextlib import ExitStack

import concourse.mybir as mybir
from concourse.masks import make_identity

F32 = mybir.dt.float32
BF16 = mybir.dt.bfloat16
I32 = mybir.dt.int32
U32 = mybir.dt.uint32
U8 = mybir.dt.uint8
FP8X4 = mybir.dt.float8_e4m3fn_x4

P = 128
PACK = 4
K_PASS = P * PACK

SEQS, FRAMES, FEATURES, SLOTS = 4, 512, 1024, 128
HALVES = FEATURES // K_PASS
UNITS = SEQS * HALVES
PAIRS = K_PASS // 2

SCALAR_SHARE = [128] + 5 * [48] + 2 * [96]
RUN = 4

BIAS_COPIES = 8

FLOPS = 2 * (2 * SEQS * FRAMES * FEATURES * SLOTS)


def tile_instrumentspecificslotmemory_pa_kernel(tc, H, Wr_words, Wr_scales, br, out):
    nc = tc.nc
    with ExitStack() as ctx:
        const = ctx.enter_context(tc.tile_pool(name="const", bufs=1))
        per_unit = ctx.enter_context(tc.tile_pool(name="per_unit", bufs=UNITS))
        per_seq = ctx.enter_context(tc.tile_pool(name="per_seq", bufs=SEQS))
        psum_t = ctx.enter_context(tc.psum_pool(name="psum_t", bufs=4))
        psum_l = ctx.enter_context(tc.psum_pool(name="psum_l", bufs=2))
        psum_r = ctx.enter_context(tc.psum_pool(name="psum_r", bufs=1))

        ctx.enter_context(tc.manual_schedule())

        identity = const.tile([P, P], F32)
        make_identity(nc, identity[:])

        zero = const.tile([P, 1], F32)
        half = const.tile([P, 1], F32)
        nc.vector.memset(zero[:], 0.0)
        nc.scalar.activation(out=half[:], in_=zero[:], func=mybir.ActivationFunctionType.Sigmoid)

        w_codes = const.tile([P, HALVES, SLOTS], U32, align_bytes=64)
        w_scales = const.tile([P, HALVES, SLOTS], U8, align_bytes=64)
        nc.vector.memset(w_scales[:].bitcast(I32), 0)

        bias_row = const.tile([P, SLOTS], BF16)
        ones = const.tile([P, P], BF16)
        nc.vector.memset(ones[:], 1.0)
        nc.vector.memset(bias_row[:], 0.0)
        nc.scalar.dma_start(out=bias_row[0:1, :], in_=br.unsqueeze(0))
        turned = psum_r.tile([SLOTS, BIAS_COPIES], F32, name="bias_turned", tag="turned")
        bias = const.tile([SLOTS, BIAS_COPIES], F32)

        def keep_warm(count, banks=psum_r, tag="unused"):
            for i in range(count):
                unused = banks.tile([P, K_PASS], F32, name="unused", tag=tag)
                nc.tensor.matmul(
                    out=unused[:], lhsT=ones[:], rhs=ones[:, 0:1].to_broadcast([P, K_PASS]), start=True, stop=True
                )

        def keep_warm_mx(count):
            w_columns = HALVES * SLOTS
            for i in range(count):
                unused = psum_r.tile([P, K_PASS], F32, name="unused")
                nc.tensor.matmul_mx(
                    out=unused[:, :w_columns],
                    lhsT=w_codes[:, 0, :].bitcast(FP8X4),
                    lhsT_scale=w_scales[:, 0, :],
                    rhs=w_codes[:].rearrange("p g n -> p (g n)").bitcast(FP8X4),
                    rhs_scale=w_scales[:].rearrange("p g n -> p (g n)"),
                    start=True,
                    stop=True,
                )

        def turn_bias():
            nc.tensor.matmul(out=turned[:], lhsT=bias_row[:], rhs=ones[:, :BIAS_COPIES], start=True, stop=True)
            nc.vector.tensor_copy(out=bias[:], in_=turned[:])

        hidden = []
        for unit in range(UNITS):
            b, g = divmod(unit, HALVES)
            h = per_unit.tile([P, PACK, K_PASS], BF16, name="h")
            piece = K_PASS // 2 if unit == 0 else K_PASS
            for first in range(0, K_PASS, piece):
                nc.sync.dma_start(
                    out=h[:, :, first : first + piece],
                    in_=H[b].rearrange("(p j) d -> p j d", j=PACK)[
                        :, :, g * K_PASS + first : g * K_PASS + first + piece
                    ],
                )
            hidden.append(h)
            if unit == 1:
                nc.sync.dma_start(
                    out=w_codes[:].bitcast(I32),
                    in_=Wr_words.rearrange("g p n t -> p g (n t)").bitcast(I32),
                )
                for quad in range(4):
                    nc.sync.dma_start(
                        out=w_scales[32 * quad : 32 * quad + 4, :, :].bitcast(I32),
                        in_=Wr_scales[:, 4 * quad : 4 * quad + 4, :].rearrange("g r n -> r g n").bitcast(I32),
                    )

        by_feature, feature_operands = [], []

        def turn_unit(unit):
            words = hidden[unit][:].bitcast(F32)
            grouped = per_unit.tile([P, PACK, P, PACK], BF16, name="by_feature", align_bytes=64)
            for first_j in range(0, PACK, 2):
                flipped = psum_t.tile([P, 2, 2, P], F32, name="flipped")
                for j in range(2):
                    for w in range(2):
                        nc.tensor.transpose(flipped[:, j, w, :], words[:, first_j + j, w:PAIRS:2], identity[:])
                nc.scalar.copy(
                    out=grouped[:, first_j : first_j + 2, :, :].bitcast(F32),
                    in_=flipped[:].rearrange("p j w f -> p j f w"),
                )
            by_feature.append(grouped)

        def quantise_along_features(unit):
            codes = per_unit.tile([P, PACK * P], U32, name="feature_codes", align_bytes=64)
            scales = per_unit.tile([P, PACK * P], U8, name="feature_scales", align_bytes=64)
            nc.vector.quantize_mx(
                out=codes[:].bitcast(FP8X4),
                scales=scales[:],
                in_=by_feature[unit][:].rearrange("p j f t -> p (j f t)"),
            )
            feature_operands.append((codes, scales))

        logits_of, by_slot_of, turned_of, route_of, route_operands = [], [], [], [], []

        def multiply_by_w(b, g):
            if g == 0:
                logits = psum_l.tile([SLOTS, PACK, P], F32, name="logits")
                logits_of.append(logits)
            codes, scales = feature_operands[b * HALVES + g]
            nc.tensor.matmul_mx(
                out=logits_of[b][:].rearrange("s j p -> s (j p)"),
                lhsT=w_codes[:, g, :].bitcast(FP8X4),
                lhsT_scale=w_scales[:, g, :],
                rhs=codes[:].bitcast(FP8X4),
                rhs_scale=scales[:],
                start=(g == 0),
                stop=(g == HALVES - 1),
            )

        def sigmoid(b):
            by_slot = per_seq.tile([SLOTS, 2, P, 2], BF16, name="by_slot")
            nc.scalar.activation(
                out=by_slot[:],
                in_=logits_of[b][:].rearrange("s (u e) p -> s u p e", u=2),
                func=mybir.ActivationFunctionType.Sigmoid,
                bias=bias[:, 0:1],
            )
            by_slot_of.append(by_slot)

        def turn_route(b):
            words = by_slot_of[b][:].rearrange("s u p e -> s (u p e)").bitcast(F32)
            turned = psum_r.tile([P, 2, SLOTS], F32, name="turned", tag="turned")
            for u in range(2):
                nc.tensor.transpose(turned[:, u, :], words[:, u * P : (u + 1) * P], identity[:])
            turned_of.append(turned)

        def fetch_route(b):
            route = per_seq.tile([P, SLOTS, PACK], BF16, name="route", align_bytes=64)
            nc.scalar.copy(
                out=route[:].rearrange("p s j -> p (s j)").bitcast(F32).rearrange("p (s u) -> p s u", u=2),
                in_=turned_of[b][:].rearrange("p u s -> p s u"),
            )
            route_of.append(route)

        def quantise_route(b):
            codes = per_seq.tile([P, SLOTS], U32, name="route_codes", align_bytes=64)
            scales = per_seq.tile([P, SLOTS], U8, name="route_scales", align_bytes=64)
            nc.vector.quantize_mx(
                out=codes[:].bitcast(FP8X4),
                scales=scales[:],
                in_=route_of[b][:].rearrange("p s j -> p (s j)"),
            )
            route_operands.append((codes, scales))

        by_frame, frame_operands = [], []

        def regroup(engine_copy, grouped, h, first, count):
            engine_copy(
                out=grouped[:, first : first + count, :].rearrange("p (c i) j -> p c j i", i=RUN),
                in_=h[:, :, first : first + count].rearrange("p j (c i) -> p c j i", i=RUN),
            )

        def regroup_on_vector(unit):
            grouped = per_unit.tile([P, K_PASS, PACK], BF16, name="by_frame", align_bytes=64)
            share = K_PASS - SCALAR_SHARE[unit]
            piece = K_PASS // 2 if unit == 0 else share
            for first in range(0, share, piece):
                regroup(nc.vector.tensor_copy, grouped, hidden[unit], first, min(piece, share - first))
            by_frame.append(grouped)

        def regroup_on_scalar(unit):
            share = SCALAR_SHARE[unit]
            regroup(nc.scalar.copy, by_frame[unit], hidden[unit], K_PASS - share, share)

        def quantise_along_frames(unit, pieces=1):
            codes = per_unit.tile([P, K_PASS], U32, name="frame_codes", align_bytes=64)
            scales = per_unit.tile([P, K_PASS], U8, name="frame_scales", align_bytes=64)
            width = K_PASS // pieces
            for first in range(0, K_PASS, width):
                nc.vector.quantize_mx(
                    out=codes[:, first : first + width].bitcast(FP8X4),
                    scales=scales[:, first : first + width],
                    in_=by_frame[unit][:, first : first + width, :].rearrange("p d j -> p (d j)"),
                )
            frame_operands.append((codes, scales))

        def pool(unit, engine_copy, first=0, count=K_PASS):
            b, g = divmod(unit, HALVES)
            columns = slice(first, first + count)
            route_codes, route_scales = route_operands[b]
            codes, scales = frame_operands[unit]
            pooled = psum_t.tile([SLOTS, K_PASS], F32, name="pooled", tag="flipped")
            nc.tensor.matmul_mx(
                out=pooled[:, :count],
                lhsT=route_codes[:].bitcast(FP8X4),
                lhsT_scale=route_scales[:],
                rhs=codes[:, columns].bitcast(FP8X4),
                rhs_scale=scales[:, columns],
                start=True,
                stop=True,
            )
            result = per_unit.tile([SLOTS, K_PASS], F32, name="result")
            engine_copy(out=result[:, :count], in_=pooled[:, :count])
            nc.sync.dma_start(out=out[b, :, g * K_PASS + first : g * K_PASS + first + count], in_=result[:, :count])

        keep_warm(4, psum_t, "flipped")
        regroup_on_vector(0)
        regroup_on_scalar(0)
        turn_unit(0)
        keep_warm(1)
        regroup_on_vector(1)
        turn_unit(1)
        regroup_on_scalar(1)
        turn_bias()
        keep_warm(1)
        for b in range(SEQS):
            quantise_along_features(2 * b)
            quantise_along_frames(b)
            quantise_along_features(2 * b + 1)
            if b >= 2:
                fetch_route(b - 2)
                quantise_route(b - 2)
            if b >= 1:
                sigmoid(b - 1)
            if b < SEQS - 1:
                turn_unit(2 * b + 2)
                multiply_by_w(b, 0)
                if b >= 1:
                    keep_warm_mx(1)
                regroup_on_vector(b + 2)
                regroup_on_scalar(b + 2)
                turn_unit(2 * b + 3)
            else:
                pool(0, nc.scalar.copy)
                multiply_by_w(b, 0)
                pool(1, nc.scalar.copy)
                regroup_on_vector(5)
                regroup_on_scalar(5)
            if b >= 1:
                turn_route(b - 1)
            multiply_by_w(b, 1)
            if b < SEQS - 1:
                keep_warm_mx(1)

        quantise_along_frames(4)
        fetch_route(2)
        sigmoid(3)
        regroup_on_vector(6)
        regroup_on_scalar(6)
        quantise_route(2)
        pool(2, nc.scalar.copy)
        pool(3, nc.scalar.copy)
        quantise_along_frames(5)
        turn_route(3)
        keep_warm_mx(2)
        fetch_route(3)
        regroup_on_vector(7)
        regroup_on_scalar(7)
        quantise_route(3)
        pool(4, nc.scalar.copy)
        pool(5, nc.scalar.copy)
        keep_warm_mx(2)
        quantise_along_frames(6)
        pool(6, nc.scalar.copy)
        quantise_along_frames(7, pieces=2)
        pool(7, nc.scalar.copy, 0, K_PASS // 2)
        pool(7, nc.vector.tensor_copy, K_PASS // 2, K_PASS // 2)
